import numpy as np
import ml_dtypes

BF16 = ml_dtypes.bfloat16


def bf(x):
    return np.asarray(x, np.float32).astype(BF16)


def f32(x):
    return np.asarray(x, np.float32)


def f64(x):
    return np.asarray(x).astype(np.float64)


def striped(idx):
    return np.tile(idx.reshape(-1, 16).T, (8, 1))


D, S, H, L, N = 128, 512, 256, 128, 128


def setup_inputs():
    return {"x": bf(np.random.uniform(0.0, 1.0, (D, S))), "w1": bf(1.5 * np.random.standard_normal((D, H)) / np.sqrt(D)), "b1": f32(0.1 * np.random.standard_normal((H, 1))), "w21": bf(np.random.standard_normal((H, L)) / np.sqrt(H)), "b21": f32(0.1 * np.random.standard_normal((L, 1))), "offs": striped(np.random.permutation(S)[:N])}


def reference(x, w1, b1, w21, b21, offs):
    idx = offs[:16].T.reshape(-1)
    h1 = np.tanh(f64(w1).T @ f64(x)[:, idx] + f64(b1))
    return f64(w21).T @ h1 + f64(b21)

@@ -1,0 +1,64 @@
+import concourse.mybir as mybir
+
+P = 128
+D, S, H, L, N = 128, 512, 256, 128, 128
+H_BLOCKS = H // P
+
+BF16, F32, U16 = mybir.dt.bfloat16, mybir.dt.float32, mybir.dt.uint16
+
+FLOPS = 2 * D * H * N + 2 * H * L * N
+BYTES = 2 * D * N + 2 * D * H + 4 * H + 2 * H * L + 4 * L + 2 * P * (N // 16) + 4 * L * N
+
+
+def tile_vae_ep_fullcov_kernel(tc, x, w1, b1, w21, b21, offs, out):
+    nc = tc.nc
+    with (
+        tc.tile_pool(name="held", bufs=1) as held,
+        tc.psum_pool(name="psum", bufs=1) as psum,
+    ):
+        offsets = held.tile([P, N // 16], U16, name="offsets")
+        nc.sync.dma_start(offsets[:], offs)
+        store = held.tile([D, S], BF16, name="store")
+        nc.sync.dma_start(store[:], x)
+        w1_sb = held.tile([D, H], BF16, name="w1_sb")
+        nc.scalar.dma_start(w1_sb[:], w1)
+
+        b1_cols = [held.tile([P, 1], F32, name=f"b1_col{k}") for k in range(H_BLOCKS)]
+        for k in range(H_BLOCKS):
+            nc.scalar.dma_start(b1_cols[k][:], b1[k * P : (k + 1) * P, :])
+
+        w21_blocks = [held.tile([P, L], BF16, name=f"w21_block{k}") for k in range(H_BLOCKS)]
+        for k in range(H_BLOCKS):
+            nc.gpsimd.dma_start(w21_blocks[k][:], w21[k * P : (k + 1) * P, :])
+        b21_col = held.tile([L, 1], F32, name="b21_col")
+        nc.gpsimd.dma_start(b21_col[:], b21)
+
+        h1_blocks = []
+        for k in range(H_BLOCKS):
+            hidden_ps = psum.tile([P, N], F32, name=f"hidden_ps{k}")
+            nc.tensor.matmul(
+                hidden_ps[:],
+                w1_sb[:, k * P : (k + 1) * P],
+                store[:].indirect(offsets[:]),
+                start=True,
+                stop=True,
+            )
+            h1_block = held.tile([P, N], BF16, name=f"h1_block{k}")
+            nc.scalar.activation(
+                h1_block[:], hidden_ps[:], mybir.ActivationFunctionType.Tanh, bias=b1_cols[k][:]
+            )
+            h1_blocks.append(h1_block)
+
+        latent_ps = psum.tile([L, N], F32, name="latent_ps")
+        for k in range(H_BLOCKS):
+            nc.tensor.matmul(
+                latent_ps[:],
+                w21_blocks[k][:],
+                h1_blocks[k][:],
+                start=(k == 0),
+                stop=(k == H_BLOCKS - 1),
+            )
+
+        latent = held.tile([L, N], F32, name="latent")
+        nc.vector.tensor_scalar(latent[:], latent_ps[:], b21_col[:], None, mybir.AluOpType.add)
+        nc.sync.dma_start(out, latent[:])

@@ -23,15 +23,13 @@ def tile_vae_ep_fullcov_kernel(tc, x, w1, b1, w21, b21, offs, out):
         w1_sb = held.tile([D, H], BF16, name="w1_sb")
         nc.scalar.dma_start(w1_sb[:], w1)
 
-        b1_cols = [held.tile([P, 1], F32, name=f"b1_col{k}") for k in range(H_BLOCKS)]
-        for k in range(H_BLOCKS):
-            nc.scalar.dma_start(b1_cols[k][:], b1[k * P : (k + 1) * P, :])
-
-        w21_blocks = [held.tile([P, L], BF16, name=f"w21_block{k}") for k in range(H_BLOCKS)]
-        for k in range(H_BLOCKS):
-            nc.gpsimd.dma_start(w21_blocks[k][:], w21[k * P : (k + 1) * P, :])
-        b21_col = held.tile([L, 1], F32, name="b21_col")
-        nc.gpsimd.dma_start(b21_col[:], b21)
+        b1_sb = held.tile([P, H_BLOCKS], F32, name="b1_sb")
+        with nc.allow_non_contiguous_dma(reason="a bias of 256 elements, one to a partition and block"):
+            nc.sync.dma_start(b1_sb[:], b1.rearrange("(k p) one -> p (k one)", p=P))
+        w21_sb = held.tile([P, H_BLOCKS, L], BF16, name="w21_sb")
+        nc.scalar.dma_start(w21_sb[:], w21.rearrange("(k p) l -> p k l", p=P))
+        b21_sb = held.tile([L, 1], F32, name="b21_sb")
+        nc.sync.dma_start(b21_sb[:], b21)
 
         h1_blocks = []
         for k in range(H_BLOCKS):
@@ -45,7 +43,7 @@ def tile_vae_ep_fullcov_kernel(tc, x, w1, b1, w21, b21, offs, out):
             )
             h1_block = held.tile([P, N], BF16, name=f"h1_block{k}")
             nc.scalar.activation(
-                h1_block[:], hidden_ps[:], mybir.ActivationFunctionType.Tanh, bias=b1_cols[k][:]
+                h1_block[:], hidden_ps[:], mybir.ActivationFunctionType.Tanh, bias=b1_sb[:, k : k + 1]
             )
             h1_blocks.append(h1_block)
 
@@ -53,12 +51,12 @@ def tile_vae_ep_fullcov_kernel(tc, x, w1, b1, w21, b21, offs, out):
         for k in range(H_BLOCKS):
             nc.tensor.matmul(
                 latent_ps[:],
-                w21_blocks[k][:],
+                w21_sb[:, k, :],
                 h1_blocks[k][:],
                 start=(k == 0),
                 stop=(k == H_BLOCKS - 1),
             )
 
         latent = held.tile([L, N], F32, name="latent")
-        nc.vector.tensor_scalar(latent[:], latent_ps[:], b21_col[:], None, mybir.AluOpType.add)
+        nc.vector.tensor_scalar(latent[:], latent_ps[:], b21_sb[:], None, mybir.AluOpType.add)
         nc.sync.dma_start(out, latent[:])

@@ -31,6 +31,10 @@ def tile_vae_ep_fullcov_kernel(tc, x, w1, b1, w21, b21, offs, out):
         b21_sb = held.tile([L, 1], F32, name="b21_sb")
         nc.sync.dma_start(b21_sb[:], b21)
 
+        warm = held.tile([P, 1], F32, name="warm")
+        nc.vector.memset(warm[:], 0.0)
+        nc.scalar.activation(warm[:], warm[:], mybir.ActivationFunctionType.Tanh)
+
         h1_blocks = []
         for k in range(H_BLOCKS):
             hidden_ps = psum.tile([P, N], F32, name=f"hidden_ps{k}")

@@ -16,18 +16,18 @@ def tile_vae_ep_fullcov_kernel(tc, x, w1, b1, w21, b21, offs, out):
         tc.tile_pool(name="held", bufs=1) as held,
         tc.psum_pool(name="psum", bufs=1) as psum,
     ):
+        store = held.tile([D, S], BF16, name="store")
+        nc.scalar.dma_start(store[:], x)
         offsets = held.tile([P, N // 16], U16, name="offsets")
         nc.sync.dma_start(offsets[:], offs)
-        store = held.tile([D, S], BF16, name="store")
-        nc.sync.dma_start(store[:], x)
         w1_sb = held.tile([D, H], BF16, name="w1_sb")
-        nc.scalar.dma_start(w1_sb[:], w1)
+        nc.sync.dma_start(w1_sb[:], w1)
 
         b1_sb = held.tile([P, H_BLOCKS], F32, name="b1_sb")
         with nc.allow_non_contiguous_dma(reason="a bias of 256 elements, one to a partition and block"):
             nc.sync.dma_start(b1_sb[:], b1.rearrange("(k p) one -> p (k one)", p=P))
         w21_sb = held.tile([P, H_BLOCKS, L], BF16, name="w21_sb")
-        nc.scalar.dma_start(w21_sb[:], w21.rearrange("(k p) l -> p k l", p=P))
+        nc.sync.dma_start(w21_sb[:], w21.rearrange("(k p) l -> p k l", p=P))
         b21_sb = held.tile([L, 1], F32, name="b21_sb")
         nc.sync.dma_start(b21_sb[:], b21)
 

@@ -3,6 +3,7 @@ import concourse.mybir as mybir
 P = 128
 D, S, H, L, N = 128, 512, 256, 128, 128
 H_BLOCKS = H // P
+WARM_MATMULS = 10
 
 BF16, F32, U16 = mybir.dt.bfloat16, mybir.dt.float32, mybir.dt.uint16
 
@@ -16,24 +17,30 @@ def tile_vae_ep_fullcov_kernel(tc, x, w1, b1, w21, b21, offs, out):
         tc.tile_pool(name="held", bufs=1) as held,
         tc.psum_pool(name="psum", bufs=1) as psum,
     ):
-        store = held.tile([D, S], BF16, name="store")
-        nc.scalar.dma_start(store[:], x)
         offsets = held.tile([P, N // 16], U16, name="offsets")
         nc.sync.dma_start(offsets[:], offs)
+        store = held.tile([D, S], BF16, name="store")
+        nc.sync.dma_start(store[:], x)
         w1_sb = held.tile([D, H], BF16, name="w1_sb")
-        nc.sync.dma_start(w1_sb[:], w1)
+        nc.scalar.dma_start(w1_sb[:], w1)
 
         b1_sb = held.tile([P, H_BLOCKS], F32, name="b1_sb")
         with nc.allow_non_contiguous_dma(reason="a bias of 256 elements, one to a partition and block"):
             nc.sync.dma_start(b1_sb[:], b1.rearrange("(k p) one -> p (k one)", p=P))
         w21_sb = held.tile([P, H_BLOCKS, L], BF16, name="w21_sb")
-        nc.sync.dma_start(w21_sb[:], w21.rearrange("(k p) l -> p k l", p=P))
+        nc.scalar.dma_start(w21_sb[:], w21.rearrange("(k p) l -> p k l", p=P))
         b21_sb = held.tile([L, 1], F32, name="b21_sb")
         nc.sync.dma_start(b21_sb[:], b21)
 
         warm = held.tile([P, 1], F32, name="warm")
         nc.vector.memset(warm[:], 0.0)
         nc.scalar.activation(warm[:], warm[:], mybir.ActivationFunctionType.Tanh)
+
+        zeros = held.tile([P, P], BF16, name="zeros")
+        nc.vector.memset(zeros[:], 0.0)
+        warm_ps = psum.tile([P, P], F32, name="warm_ps")
+        for i in range(WARM_MATMULS):
+            nc.tensor.matmul(warm_ps[:], zeros[:], zeros[:], start=True, stop=True)
 
         h1_blocks = []
         for k in range(H_BLOCKS):

@@ -3,7 +3,6 @@ import concourse.mybir as mybir
 P = 128
 D, S, H, L, N = 128, 512, 256, 128, 128
 H_BLOCKS = H // P
-WARM_MATMULS = 10
 
 BF16, F32, U16 = mybir.dt.bfloat16, mybir.dt.float32, mybir.dt.uint16
 
@@ -22,25 +21,19 @@ def tile_vae_ep_fullcov_kernel(tc, x, w1, b1, w21, b21, offs, out):
         store = held.tile([D, S], BF16, name="store")
         nc.sync.dma_start(store[:], x)
         w1_sb = held.tile([D, H], BF16, name="w1_sb")
-        nc.scalar.dma_start(w1_sb[:], w1)
+        nc.sync.dma_start(w1_sb[:], w1)
 
         b1_sb = held.tile([P, H_BLOCKS], F32, name="b1_sb")
         with nc.allow_non_contiguous_dma(reason="a bias of 256 elements, one to a partition and block"):
             nc.sync.dma_start(b1_sb[:], b1.rearrange("(k p) one -> p (k one)", p=P))
         w21_sb = held.tile([P, H_BLOCKS, L], BF16, name="w21_sb")
-        nc.scalar.dma_start(w21_sb[:], w21.rearrange("(k p) l -> p k l", p=P))
+        nc.sync.dma_start(w21_sb[:], w21.rearrange("(k p) l -> p k l", p=P))
         b21_sb = held.tile([L, 1], F32, name="b21_sb")
         nc.sync.dma_start(b21_sb[:], b21)
 
         warm = held.tile([P, 1], F32, name="warm")
         nc.vector.memset(warm[:], 0.0)
         nc.scalar.activation(warm[:], warm[:], mybir.ActivationFunctionType.Tanh)
-
-        zeros = held.tile([P, P], BF16, name="zeros")
-        nc.vector.memset(zeros[:], 0.0)
-        warm_ps = psum.tile([P, P], F32, name="warm_ps")
-        for i in range(WARM_MATMULS):
-            nc.tensor.matmul(warm_ps[:], zeros[:], zeros[:], start=True, stop=True)
 
         h1_blocks = []
         for k in range(H_BLOCKS):

@@ -21,13 +21,13 @@ def tile_vae_ep_fullcov_kernel(tc, x, w1, b1, w21, b21, offs, out):
         store = held.tile([D, S], BF16, name="store")
         nc.sync.dma_start(store[:], x)
         w1_sb = held.tile([D, H], BF16, name="w1_sb")
-        nc.sync.dma_start(w1_sb[:], w1)
+        nc.scalar.dma_start(w1_sb[:], w1)
 
         b1_sb = held.tile([P, H_BLOCKS], F32, name="b1_sb")
         with nc.allow_non_contiguous_dma(reason="a bias of 256 elements, one to a partition and block"):
-            nc.sync.dma_start(b1_sb[:], b1.rearrange("(k p) one -> p (k one)", p=P))
+            nc.scalar.dma_start(b1_sb[:], b1.rearrange("(k p) one -> p (k one)", p=P))
         w21_sb = held.tile([P, H_BLOCKS, L], BF16, name="w21_sb")
-        nc.sync.dma_start(w21_sb[:], w21.rearrange("(k p) l -> p k l", p=P))
+        nc.scalar.dma_start(w21_sb[:], w21.rearrange("(k p) l -> p k l", p=P))
         b21_sb = held.tile([L, 1], F32, name="b21_sb")
         nc.sync.dma_start(b21_sb[:], b21)
 

@@ -16,10 +16,10 @@ def tile_vae_ep_fullcov_kernel(tc, x, w1, b1, w21, b21, offs, out):
         tc.tile_pool(name="held", bufs=1) as held,
         tc.psum_pool(name="psum", bufs=1) as psum,
     ):
-        offsets = held.tile([P, N // 16], U16, name="offsets")
-        nc.sync.dma_start(offsets[:], offs)
         store = held.tile([D, S], BF16, name="store")
         nc.sync.dma_start(store[:], x)
+        offsets = held.tile([P, N // 16], U16, name="offsets")
+        nc.sync.dma_start(offsets[:], offs)
         w1_sb = held.tile([D, H], BF16, name="w1_sb")
         nc.scalar.dma_start(w1_sb[:], w1)
 

@@ -17,11 +17,11 @@ def tile_vae_ep_fullcov_kernel(tc, x, w1, b1, w21, b21, offs, out):
         tc.psum_pool(name="psum", bufs=1) as psum,
     ):
         store = held.tile([D, S], BF16, name="store")
-        nc.sync.dma_start(store[:], x)
+        nc.scalar.dma_start(store[:], x)
         offsets = held.tile([P, N // 16], U16, name="offsets")
         nc.sync.dma_start(offsets[:], offs)
         w1_sb = held.tile([D, H], BF16, name="w1_sb")
-        nc.scalar.dma_start(w1_sb[:], w1)
+        nc.sync.dma_start(w1_sb[:], w1)
 
         b1_sb = held.tile([P, H_BLOCKS], F32, name="b1_sb")
         with nc.allow_non_contiguous_dma(reason="a bias of 256 elements, one to a partition and block"):

@@ -24,10 +24,9 @@ def tile_vae_ep_fullcov_kernel(tc, x, w1, b1, w21, b21, offs, out):
         nc.sync.dma_start(w1_sb[:], w1)
 
         b1_sb = held.tile([P, H_BLOCKS], F32, name="b1_sb")
-        with nc.allow_non_contiguous_dma(reason="a bias of 256 elements, one to a partition and block"):
-            nc.scalar.dma_start(b1_sb[:], b1.rearrange("(k p) one -> p (k one)", p=P))
+        nc.scalar.dma_start(b1_sb[:], b1.rearrange("(p k) one -> p (k one)", p=P))
         w21_sb = held.tile([P, H_BLOCKS, L], BF16, name="w21_sb")
-        nc.scalar.dma_start(w21_sb[:], w21.rearrange("(k p) l -> p k l", p=P))
+        nc.scalar.dma_start(w21_sb[:], w21.rearrange("(p k) l -> p k l", p=P))
         b21_sb = held.tile([L, 1], F32, name="b21_sb")
         nc.sync.dma_start(b21_sb[:], b21)
 
@@ -40,7 +39,7 @@ def tile_vae_ep_fullcov_kernel(tc, x, w1, b1, w21, b21, offs, out):
             hidden_ps = psum.tile([P, N], F32, name=f"hidden_ps{k}")
             nc.tensor.matmul(
                 hidden_ps[:],
-                w1_sb[:, k * P : (k + 1) * P],
+                w1_sb[:, k::H_BLOCKS],
                 store[:].indirect(offsets[:]),
                 start=True,
                 stop=True,

@@ -3,6 +3,8 @@ import concourse.mybir as mybir
 P = 128
 D, S, H, L, N = 128, 512, 256, 128, 128
 H_BLOCKS = H // P
+HALVES = 2
+HALF = N // HALVES
 
 BF16, F32, U16 = mybir.dt.bfloat16, mybir.dt.float32, mybir.dt.uint16
 
@@ -45,21 +47,30 @@ def tile_vae_ep_fullcov_kernel(tc, x, w1, b1, w21, b21, offs, out):
                 stop=True,
             )
             h1_block = held.tile([P, N], BF16, name=f"h1_block{k}")
-            nc.scalar.activation(
-                h1_block[:], hidden_ps[:], mybir.ActivationFunctionType.Tanh, bias=b1_sb[:, k : k + 1]
-            )
+            width = HALF if k == H_BLOCKS - 1 else N
+            for a in range(0, N, width):
+                nc.scalar.activation(
+                    h1_block[:, a : a + width],
+                    hidden_ps[:, a : a + width],
+                    mybir.ActivationFunctionType.Tanh,
+                    bias=b1_sb[:, k : k + 1],
+                )
             h1_blocks.append(h1_block)
 
-        latent_ps = psum.tile([L, N], F32, name="latent_ps")
+        latent_ps = [psum.tile([L, HALF], F32, name=f"latent_ps{a}") for a in range(HALVES)]
         for k in range(H_BLOCKS):
-            nc.tensor.matmul(
-                latent_ps[:],
-                w21_sb[:, k, :],
-                h1_blocks[k][:],
-                start=(k == 0),
-                stop=(k == H_BLOCKS - 1),
-            )
+            for a in range(HALVES):
+                nc.tensor.matmul(
+                    latent_ps[a][:],
+                    w21_sb[:, k, :],
+                    h1_blocks[k][:, a * HALF : (a + 1) * HALF],
+                    start=(k == 0),
+                    stop=(k == H_BLOCKS - 1),
+                )
 
         latent = held.tile([L, N], F32, name="latent")
-        nc.vector.tensor_scalar(latent[:], latent_ps[:], b21_sb[:], None, mybir.AluOpType.add)
+        for a in range(HALVES):
+            nc.vector.tensor_scalar(
+                latent[:, a * HALF : (a + 1) * HALF], latent_ps[a][:], b21_sb[:], None, mybir.AluOpType.add
+            )
         nc.sync.dma_start(out, latent[:])

@@ -19,11 +19,11 @@ def tile_vae_ep_fullcov_kernel(tc, x, w1, b1, w21, b21, offs, out):
         tc.psum_pool(name="psum", bufs=1) as psum,
     ):
         store = held.tile([D, S], BF16, name="store")
-        nc.scalar.dma_start(store[:], x)
+        nc.sync.dma_start(store[:], x)
         offsets = held.tile([P, N // 16], U16, name="offsets")
         nc.sync.dma_start(offsets[:], offs)
         w1_sb = held.tile([D, H], BF16, name="w1_sb")
-        nc.sync.dma_start(w1_sb[:], w1)
+        nc.scalar.dma_start(w1_sb[:], w1)
 
         b1_sb = held.tile([P, H_BLOCKS], F32, name="b1_sb")
         nc.scalar.dma_start(b1_sb[:], b1.rearrange("(p k) one -> p (k one)", p=P))

@@ -24,13 +24,12 @@ def tile_vae_ep_fullcov_kernel(tc, x, w1, b1, w21, b21, offs, out):
         nc.sync.dma_start(offsets[:], offs)
         w1_sb = held.tile([D, H], BF16, name="w1_sb")
         nc.scalar.dma_start(w1_sb[:], w1)
-
         b1_sb = held.tile([P, H_BLOCKS], F32, name="b1_sb")
         nc.scalar.dma_start(b1_sb[:], b1.rearrange("(p k) one -> p (k one)", p=P))
         w21_sb = held.tile([P, H_BLOCKS, L], BF16, name="w21_sb")
-        nc.scalar.dma_start(w21_sb[:], w21.rearrange("(p k) l -> p k l", p=P))
+        nc.sync.dma_start(w21_sb[:], w21.rearrange("(p k) l -> p k l", p=P))
         b21_sb = held.tile([L, 1], F32, name="b21_sb")
-        nc.sync.dma_start(b21_sb[:], b21)
+        nc.scalar.dma_start(b21_sb[:], b21)
 
         warm = held.tile([P, 1], F32, name="warm")
         nc.vector.memset(warm[:], 0.0)

@@ -5,6 +5,7 @@ D, S, H, L, N = 128, 512, 256, 128, 128
 H_BLOCKS = H // P
 HALVES = 2
 HALF = N // HALVES
+DMA_BURST = 256
 
 BF16, F32, U16 = mybir.dt.bfloat16, mybir.dt.float32, mybir.dt.uint16
 
@@ -18,15 +19,15 @@ def tile_vae_ep_fullcov_kernel(tc, x, w1, b1, w21, b21, offs, out):
         tc.tile_pool(name="held", bufs=1) as held,
         tc.psum_pool(name="psum", bufs=1) as psum,
     ):
-        store = held.tile([D, S], BF16, name="store")
+        store = held.tile([D, S], BF16, name="store", align_bytes=DMA_BURST)
         nc.sync.dma_start(store[:], x)
         offsets = held.tile([P, N // 16], U16, name="offsets")
         nc.sync.dma_start(offsets[:], offs)
-        w1_sb = held.tile([D, H], BF16, name="w1_sb")
+        w1_sb = held.tile([D, H], BF16, name="w1_sb", align_bytes=DMA_BURST)
         nc.scalar.dma_start(w1_sb[:], w1)
         b1_sb = held.tile([P, H_BLOCKS], F32, name="b1_sb")
         nc.scalar.dma_start(b1_sb[:], b1.rearrange("(p k) one -> p (k one)", p=P))
-        w21_sb = held.tile([P, H_BLOCKS, L], BF16, name="w21_sb")
+        w21_sb = held.tile([P, H_BLOCKS, L], BF16, name="w21_sb", align_bytes=DMA_BURST)
         nc.sync.dma_start(w21_sb[:], w21.rearrange("(p k) l -> p k l", p=P))
         b21_sb = held.tile([L, 1], F32, name="b21_sb")
         nc.scalar.dma_start(b21_sb[:], b21)
@@ -67,7 +68,7 @@ def tile_vae_ep_fullcov_kernel(tc, x, w1, b1, w21, b21, offs, out):
                     stop=(k == H_BLOCKS - 1),
                 )
 
-        latent = held.tile([L, N], F32, name="latent")
+        latent = held.tile([L, N], F32, name="latent", align_bytes=DMA_BURST)
         for a in range(HALVES):
             nc.vector.tensor_scalar(
                 latent[:, a * HALF : (a + 1) * HALF], latent_ps[a][:], b21_sb[:], None, mybir.AluOpType.add

@@ -5,7 +5,7 @@ D, S, H, L, N = 128, 512, 256, 128, 128
 H_BLOCKS = H // P
 HALVES = 2
 HALF = N // HALVES
-DMA_BURST = 256
+ROW_ALIGN = 512
 
 BF16, F32, U16 = mybir.dt.bfloat16, mybir.dt.float32, mybir.dt.uint16
 
@@ -19,15 +19,15 @@ def tile_vae_ep_fullcov_kernel(tc, x, w1, b1, w21, b21, offs, out):
         tc.tile_pool(name="held", bufs=1) as held,
         tc.psum_pool(name="psum", bufs=1) as psum,
     ):
-        store = held.tile([D, S], BF16, name="store", align_bytes=DMA_BURST)
+        store = held.tile([D, S], BF16, name="store", align_bytes=ROW_ALIGN)
         nc.sync.dma_start(store[:], x)
         offsets = held.tile([P, N // 16], U16, name="offsets")
         nc.sync.dma_start(offsets[:], offs)
-        w1_sb = held.tile([D, H], BF16, name="w1_sb", align_bytes=DMA_BURST)
+        w1_sb = held.tile([D, H], BF16, name="w1_sb", align_bytes=ROW_ALIGN)
         nc.scalar.dma_start(w1_sb[:], w1)
         b1_sb = held.tile([P, H_BLOCKS], F32, name="b1_sb")
         nc.scalar.dma_start(b1_sb[:], b1.rearrange("(p k) one -> p (k one)", p=P))
-        w21_sb = held.tile([P, H_BLOCKS, L], BF16, name="w21_sb", align_bytes=DMA_BURST)
+        w21_sb = held.tile([P, H_BLOCKS, L], BF16, name="w21_sb", align_bytes=ROW_ALIGN)
         nc.sync.dma_start(w21_sb[:], w21.rearrange("(p k) l -> p k l", p=P))
         b21_sb = held.tile([L, 1], F32, name="b21_sb")
         nc.scalar.dma_start(b21_sb[:], b21)
@@ -46,7 +46,7 @@ def tile_vae_ep_fullcov_kernel(tc, x, w1, b1, w21, b21, offs, out):
                 start=True,
                 stop=True,
             )
-            h1_block = held.tile([P, N], BF16, name=f"h1_block{k}")
+            h1_block = held.tile([P, N], BF16, name=f"h1_block{k}", align_bytes=ROW_ALIGN)
             width = HALF if k == H_BLOCKS - 1 else N
             for a in range(0, N, width):
                 nc.scalar.activation(
@@ -68,7 +68,7 @@ def tile_vae_ep_fullcov_kernel(tc, x, w1, b1, w21, b21, offs, out):
                     stop=(k == H_BLOCKS - 1),
                 )
 
-        latent = held.tile([L, N], F32, name="latent", align_bytes=DMA_BURST)
+        latent = held.tile([L, N], F32, name="latent", align_bytes=ROW_ALIGN)
         for a in range(HALVES):
             nc.vector.tensor_scalar(
                 latent[:, a * HALF : (a + 1) * HALF], latent_ps[a][:], b21_sb[:], None, mybir.AluOpType.add

import concourse.mybir as mybir

P = 128
D, S, H, L, N = 128, 512, 256, 128, 128
H_BLOCKS = H // P
HALVES = 2
HALF = N // HALVES
ROW_ALIGN = 512

BF16, F32, U16 = mybir.dt.bfloat16, mybir.dt.float32, mybir.dt.uint16

FLOPS = 2 * D * H * N + 2 * H * L * N
BYTES = 2 * D * N + 2 * D * H + 4 * H + 2 * H * L + 4 * L + 2 * P * (N // 16) + 4 * L * N


def tile_vae_ep_fullcov_kernel(tc, x, w1, b1, w21, b21, offs, out):
    nc = tc.nc
    with (
        tc.tile_pool(name="held", bufs=1) as held,
        tc.psum_pool(name="psum", bufs=1) as psum,
    ):
        store = held.tile([D, S], BF16, name="store", align_bytes=ROW_ALIGN)
        nc.sync.dma_start(store[:], x)
        offsets = held.tile([P, N // 16], U16, name="offsets")
        nc.sync.dma_start(offsets[:], offs)
        w1_sb = held.tile([D, H], BF16, name="w1_sb", align_bytes=ROW_ALIGN)
        nc.scalar.dma_start(w1_sb[:], w1)
        b1_sb = held.tile([P, H_BLOCKS], F32, name="b1_sb")
        nc.scalar.dma_start(b1_sb[:], b1.rearrange("(p k) one -> p (k one)", p=P))
        w21_sb = held.tile([P, H_BLOCKS, L], BF16, name="w21_sb", align_bytes=ROW_ALIGN)
        nc.sync.dma_start(w21_sb[:], w21.rearrange("(p k) l -> p k l", p=P))
        b21_sb = held.tile([L, 1], F32, name="b21_sb")
        nc.scalar.dma_start(b21_sb[:], b21)

        warm = held.tile([P, 1], F32, name="warm")
        nc.vector.memset(warm[:], 0.0)
        nc.scalar.activation(warm[:], warm[:], mybir.ActivationFunctionType.Tanh)

        h1_blocks = []
        for k in range(H_BLOCKS):
            hidden_ps = psum.tile([P, N], F32, name=f"hidden_ps{k}")
            nc.tensor.matmul(
                hidden_ps[:],
                w1_sb[:, k::H_BLOCKS],
                store[:].indirect(offsets[:]),
                start=True,
                stop=True,
            )
            h1_block = held.tile([P, N], BF16, name=f"h1_block{k}", align_bytes=ROW_ALIGN)
            width = HALF if k == H_BLOCKS - 1 else N
            for a in range(0, N, width):
                nc.scalar.activation(
                    h1_block[:, a : a + width],
                    hidden_ps[:, a : a + width],
                    mybir.ActivationFunctionType.Tanh,
                    bias=b1_sb[:, k : k + 1],
                )
            h1_blocks.append(h1_block)

        latent_ps = [psum.tile([L, HALF], F32, name=f"latent_ps{a}") for a in range(HALVES)]
        for k in range(H_BLOCKS):
            for a in range(HALVES):
                nc.tensor.matmul(
                    latent_ps[a][:],
                    w21_sb[:, k, :],
                    h1_blocks[k][:, a * HALF : (a + 1) * HALF],
                    start=(k == 0),
                    stop=(k == H_BLOCKS - 1),
                )

        latent = held.tile([L, N], F32, name="latent", align_bytes=ROW_ALIGN)
        for a in range(HALVES):
            nc.vector.tensor_scalar(
                latent[:, a * HALF : (a + 1) * HALF], latent_ps[a][:], b21_sb[:], None, mybir.AluOpType.add
            )
        nc.sync.dma_start(out, latent[:])
